import numpy as np
import ml_dtypes


def mxq(x, axis, fmt="e4m3"):
    dtype, down = {"e4m3": (ml_dtypes.float8_e4m3fn, 7), "e5m2": (ml_dtypes.float8_e5m2, 14)}[fmt]
    v = np.moveaxis(np.asarray(x, np.float32).astype(ml_dtypes.bfloat16).astype(np.float64), axis, -1)
    blocks = v.reshape(v.shape[:-1] + (-1, 32))
    amax = np.abs(blocks).max(-1, keepdims=True)
    byte = np.maximum(np.where(amax > 0, np.frexp(amax)[1] - 1 + 127, 0) - down, 1)
    scale = np.exp2(byte - 127.0)
    codes = (blocks / scale).astype(np.float32).astype(dtype).astype(np.float64)
    return np.moveaxis((codes * scale).reshape(v.shape), -1, axis)


WIDE = False


def mx_kscale(k):
    if not WIDE:
        return np.ones(k)
    levels = np.array([20, -20, 10, -10, 0])
    a = np.random.permutation(np.resize(levels, k // 512 * 4)).reshape(k // 512, 4)
    idx = np.arange(k)
    return np.exp2(a[idx // 512, idx % 128 // 32])


BF16 = ml_dtypes.bfloat16


def bf(x):
    return np.asarray(x, np.float32).astype(BF16)


def f64(x):
    return np.asarray(x).astype(np.float64)


B, S, IN, OUT = 2, 512, 1024, 1024
T = B * S


def _hamilton_weight(r, i, j, k):
    col0 = np.concatenate([r, -i, -j, -k], axis=0)
    col1 = np.concatenate([i, r, -k, j], axis=0)
    col2 = np.concatenate([j, k, r, -i], axis=0)
    col3 = np.concatenate([k, -j, i, r], axis=0)
    return np.concatenate([col0, col1, col2, col3], axis=1)


def _stack(a, width):
    return a.reshape(T, 4, width).transpose(1, 0, 2).reshape(4 * T, width)


def setup_inputs():
    s = mx_kscale(4 * T).reshape(4, T).T.reshape(B, S, 4, 1)
    sc = 1.0 / np.sqrt(2 * IN)
    x = (np.random.standard_normal((B, S, 4, IN)) * s).reshape(B, S, 4 * IN)
    r = np.random.standard_normal((IN, OUT)) * sc
    i = np.random.standard_normal((IN, OUT)) * sc
    j = np.random.standard_normal((IN, OUT)) * sc
    k = np.random.standard_normal((IN, OUT)) * sc
    b = np.random.standard_normal(4 * OUT) * 0.5
    g = np.random.standard_normal((B, S, 4, OUT)) * np.exp2(np.random.randint(-12, 1, (B, S, 1, 1))) * 0.25 / s
    g = g.reshape(B, S, 4 * OUT)
    return {"x": bf(x), "r_weight": bf(r), "i_weight": bf(i), "j_weight": bf(j),
            "k_weight": bf(k), "bias": bf(b), "grad_out": bf(g)}


def reference(x, r_weight, i_weight, j_weight, k_weight, bias, grad_out):
    xs = _stack(f64(x), IN)
    gs = _stack(f64(grad_out), OUT)
    return mxq(xs, 0, "e4m3").T @ mxq(gs, 0, "e5m2")

@@ -1,0 +1,231 @@
+from contextlib import ExitStack
+
+import concourse.mybir as mybir
+
+BF16 = mybir.dt.bfloat16
+F32 = mybir.dt.float32
+U32 = mybir.dt.uint32
+U8 = mybir.dt.uint8
+E4M3 = mybir.dt.float8_e4m3fn_x4
+E5M2 = mybir.dt.float8_e5m2_x4
+
+P = 128
+J = 4
+W = 512
+FEAT = 1024
+PASSES = 8
+MT = 4
+NT = 2
+
+FLOPS = 2 * 4096 * 1024 * 1024
+BYTES = 2 * (1024 * 4096 * 2) + 1024 * 1024 * 4
+
+PIN = True
+FS = 264
+FS_END = 176
+GRP_BUFS = 5
+K_OUTER2 = 5
+
+
+def tile_qlinear_kernel(tc, x, r_weight, i_weight, j_weight, k_weight, bias, grad_out, out):
+    nc = tc.nc
+    xv = x.rearrange("h (p j) c -> h p j c", j=J)
+    gv = grad_out.rearrange("h (p j) c -> h p j c", j=J)
+
+    with ExitStack() as ctx:
+        if PIN:
+            ctx.enter_context(tc.manual_schedule())
+        raw = ctx.enter_context(tc.tile_pool(name="raw", bufs=8))
+        stage = ctx.enter_context(tc.tile_pool(name="stage", bufs=GRP_BUFS))
+        keep = ctx.enter_context(tc.tile_pool(name="keep", bufs=1))
+        outp = ctx.enter_context(tc.tile_pool(name="outp", bufs=4))
+        psum = ctx.enter_context(tc.psum_pool(name="psum", bufs=1))
+
+        src = {}
+        grp = {}
+        codes = {}
+        scales = {}
+        acc = {}
+
+        def load_x(r, c):
+            h, q = divmod(c, 4)
+            t = raw.tile([P, J, W], BF16, name="xraw%d%d" % (r, c), tag="xraw")
+            col = q * FEAT + r * W
+            nc.sync.dma_start(out=t[:], in_=xv[h, :, :, col : col + W])
+            src[("x", r, c)] = t[:]
+
+        def load_g(c, halves):
+            h, q = divmod(c, 4)
+            t = raw.tile([P, J, FEAT], BF16, name="graw%d" % c, tag="graw")
+            col = q * FEAT
+            if halves:
+                for n in range(NT):
+                    nc.sync.dma_start(
+                        out=t[:, :, n * W : (n + 1) * W], in_=gv[h, :, :, col + n * W : col + (n + 1) * W]
+                    )
+            else:
+                nc.sync.dma_start(out=t[:], in_=gv[h, :, :, col : col + FEAT])
+            for n in range(NT):
+                src[("g", n, c)] = t[:, :, n * W : (n + 1) * W]
+
+        def nm(u):
+            return "%s%d%d" % u
+
+        def copy_part(eng, u, a, b):
+            dst = grp[u][:, a:b, :].rearrange("p (c i) t -> p c t i", i=4)
+            s = src[u][:, :, a:b].rearrange("p t (c i) -> p c t i", i=4)
+            if eng == "S":
+                nc.scalar.copy(out=dst, in_=s)
+            else:
+                nc.vector.tensor_copy(out=dst, in_=s)
+
+        def new_unit(u):
+            grp[u] = stage.tile([P, W, J], BF16, name="grp" + nm(u), tag="grp", align_bytes=64)
+            codes[u] = keep.tile([P, W], U32, name="cod" + nm(u), align_bytes=64)
+            scales[u] = keep.tile([P, W], U8, name="scl" + nm(u), align_bytes=64)
+
+        def regroup(u, fs):
+            new_unit(u)
+            copy_part("S", u, 0, fs)
+            copy_part("V", u, fs, W)
+
+        def quantise(u, a=0, b=W):
+            fmt = E4M3 if u[0] == "x" else E5M2
+            nc.vector.quantize_mx(
+                out=codes[u][:, a:b].bitcast(fmt),
+                scales=scales[u][:, a:b],
+                in_=grp[u][:, a:b, :].rearrange("p w t -> p (w t)"),
+            )
+
+        def mx_pass(r, c, m, n):
+            xu = ("x", r, c)
+            gu = ("g", n, c)
+            nc.tensor.matmul_mx(
+                out=acc[(r, m, n)][:],
+                lhsT=codes[xu][:, m * P : (m + 1) * P].bitcast(E4M3),
+                lhsT_scale=scales[xu][:, m * P : (m + 1) * P],
+                rhs=codes[gu][:].bitcast(E5M2),
+                rhs_scale=scales[gu][:],
+                start=(c == 0),
+                stop=(c == PASSES - 1),
+            )
+
+        def new_acc(r, m, n):
+            acc[(r, m, n)] = psum.tile([P, W], F32, name="acc%d%d%d" % (r, m, n), tag="acc%d%d" % (m, n))
+
+        osb = {}
+
+        def evac(eng, r, m, n):
+            if (r, m) not in osb:
+                osb[(r, m)] = outp.tile([P, NT * W], F32, name="osb%d%d" % (r, m), tag="osb")
+            dst = osb[(r, m)][:, n * W : (n + 1) * W]
+            if eng == "S":
+                nc.scalar.copy(out=dst, in_=acc[(r, m, n)][:])
+            else:
+                nc.vector.tensor_copy(out=dst, in_=acc[(r, m, n)][:])
+
+        def store(r, m, n=None):
+            row = (r * MT + m) * P
+            if n is None:
+                nc.sync.dma_start(out=out[row : row + P, :], in_=osb[(r, m)][:])
+            else:
+                nc.sync.dma_start(
+                    out=out[row : row + P, n * W : (n + 1) * W], in_=osb[(r, m)][:, n * W : (n + 1) * W]
+                )
+
+        units = []
+        for c in range(PASSES):
+            if c < PASSES - 1:
+                load_x(0, c)
+                units.append(("x", 0, c))
+            load_g(c, halves=(c == 0 or c >= PASSES - 2))
+            units.append(("g", 0, c))
+            units.append(("g", 1, c))
+        load_x(0, PASSES - 1)
+        last = ("x", 0, PASSES - 1)
+
+        for m in range(MT):
+            for n in range(NT):
+                new_acc(0, m, n)
+
+        ready = set()
+        issued = set()
+
+        def passes_now():
+            for c in range(PASSES):
+                for n in range(NT):
+                    if (c, n) not in issued and ("x", 0, c) in ready and ("g", n, c) in ready:
+                        issued.add((c, n))
+                        for m in range(MT):
+                            mx_pass(0, c, m, n)
+
+        for i, u in enumerate(units):
+            regroup(u, FS if i < len(units) - 2 else FS_END)
+            if u[0] == "x":
+                load_x(1, u[2])
+            if i >= 1:
+                quantise(units[i - 1])
+                ready.add(units[i - 1])
+                passes_now()
+
+        new_unit(last)
+        copy_part("S", last, 2 * P, W)
+        copy_part("V", last, 0, P)
+        quantise(units[-1])
+        copy_part("V", last, P, 2 * P)
+        load_x(1, PASSES - 1)
+        c7 = PASSES - 1
+        quantise(last, 0, P)
+        mx_pass(0, c7, 0, 0)
+        mx_pass(0, c7, 0, 1)
+        quantise(last, P, 2 * P)
+        mx_pass(0, c7, 1, 0)
+        mx_pass(0, c7, 1, 1)
+        quantise(last, 2 * P, W)
+        for m in (2, 3):
+            mx_pass(0, c7, m, 0)
+            mx_pass(0, c7, m, 1)
+
+        hu = [("x", 1, c) for c in range(PASSES)]
+        regroup(hu[0], FS_END)
+        evac("S", 0, 0, 0)
+        evac("V", 0, 0, 1)
+        store(0, 0)
+        quantise(hu[0])
+        evac("S", 0, 1, 0)
+        evac("V", 0, 1, 1)
+        store(0, 1)
+        regroup(hu[1], FS)
+        evac("S", 0, 2, 0)
+        evac("V", 0, 2, 1)
+        store(0, 2)
+        quantise(hu[1])
+        evac("S", 0, 3, 0)
+        evac("V", 0, 3, 1)
+        store(0, 3)
+        for m in range(MT):
+            for n in range(NT):
+                new_acc(1, m, n)
+        for c in range(2):
+            for m in range(MT):
+                for n in range(NT):
+                    mx_pass(1, c, m, n)
+
+        regroup(hu[2], FS)
+        for c in range(3, PASSES):
+            regroup(hu[c], FS)
+            quantise(hu[c - 1])
+            if c - 1 < K_OUTER2:
+                for m in range(MT):
+                    for n in range(NT):
+                        mx_pass(1, c - 1, m, n)
+        quantise(hu[PASSES - 1])
+        for m in range(MT):
+            for n in range(NT):
+                for c in range(K_OUTER2, PASSES):
+                    mx_pass(1, c, m, n)
+                evac("S" if n == 0 else "V", 1, m, n)
+                if m == MT - 1:
+                    store(1, m, n)
+            if m < MT - 1:
+                store(1, m)

@@ -16,15 +16,15 @@ FEAT = 1024
 PASSES = 8
 MT = 4
 NT = 2
+LO, HI = 0, 1
 
 FLOPS = 2 * 4096 * 1024 * 1024
 BYTES = 2 * (1024 * 4096 * 2) + 1024 * 1024 * 4
 
-PIN = True
-FS = 264
-FS_END = 176
+A = 5
+FS = 280
 GRP_BUFS = 5
-K_OUTER2 = 5
+XRAW_BUFS = 8
 
 
 def tile_qlinear_kernel(tc, x, r_weight, i_weight, j_weight, k_weight, bias, grad_out, out):
@@ -33,8 +33,7 @@ def tile_qlinear_kernel(tc, x, r_weight, i_weight, j_weight, k_weight, bias, gra
     gv = grad_out.rearrange("h (p j) c -> h p j c", j=J)
 
     with ExitStack() as ctx:
-        if PIN:
-            ctx.enter_context(tc.manual_schedule())
+        ctx.enter_context(tc.manual_schedule())
         raw = ctx.enter_context(tc.tile_pool(name="raw", bufs=8))
         stage = ctx.enter_context(tc.tile_pool(name="stage", bufs=GRP_BUFS))
         keep = ctx.enter_context(tc.tile_pool(name="keep", bufs=1))
@@ -46,27 +45,54 @@ def tile_qlinear_kernel(tc, x, r_weight, i_weight, j_weight, k_weight, bias, gra
         codes = {}
         scales = {}
         acc = {}
+        spl = {}
+        osb = {}
 
-        def load_x(r, c):
-            h, q = divmod(c, 4)
-            t = raw.tile([P, J, W], BF16, name="xraw%d%d" % (r, c), tag="xraw")
-            col = q * FEAT + r * W
-            nc.sync.dma_start(out=t[:], in_=xv[h, :, :, col : col + W])
-            src[("x", r, c)] = t[:]
-
-        def load_g(c, halves):
-            h, q = divmod(c, 4)
-            t = raw.tile([P, J, FEAT], BF16, name="graw%d" % c, tag="graw")
-            col = q * FEAT
-            if halves:
-                for n in range(NT):
-                    nc.sync.dma_start(
-                        out=t[:, :, n * W : (n + 1) * W], in_=gv[h, :, :, col + n * W : col + (n + 1) * W]
-                    )
+        units = []
+        pending = []
+        for c in range(A):
+            if c < A - 1:
+                pending.append(("x", LO, c))
+            pending.append(("g", c))
+        pending.append(("x", LO, A - 1))
+        for c in range(A):
+            pending.append(("x", HI, c))
+        for c in range(A, PASSES):
+            if c < PASSES - 1:
+                pending.append(("x", HI, c))
+            pending.append(("g", c))
+        pending.append(("x", HI, PASSES - 1))
+        for c in range(A, PASSES):
+            pending.append(("x", LO, c))
+        for ld in pending:
+            if ld[0] == "x":
+                units.append(ld)
             else:
-                nc.sync.dma_start(out=t[:], in_=gv[h, :, :, col : col + FEAT])
-            for n in range(NT):
-                src[("g", n, c)] = t[:, :, n * W : (n + 1) * W]
+                units.append(("g", 0, ld[1]))
+                units.append(("g", 1, ld[1]))
+        live = {"x": 0, "next": 0}
+
+        def pump():
+            while live["next"] < len(pending):
+                ld = pending[live["next"]]
+                if ld[0] == "x":
+                    if live["x"] == XRAW_BUFS:
+                        return
+                    live["x"] += 1
+                    r, c = ld[1], ld[2]
+                    h, q = divmod(c, 4)
+                    t = raw.tile([P, J, W], BF16, name="xraw%d%d" % (r, c), tag="xraw")
+                    col = q * FEAT + r * W
+                    nc.sync.dma_start(out=t[:], in_=xv[h, :, :, col : col + W])
+                    src[ld] = t[:]
+                else:
+                    c = ld[1]
+                    h, q = divmod(c, 4)
+                    t = raw.tile([P, J, FEAT], BF16, name="graw%d" % c, tag="graw")
+                    nc.sync.dma_start(out=t[:], in_=gv[h, :, :, q * FEAT : (q + 1) * FEAT])
+                    for n in range(NT):
+                        src[("g", n, c)] = t[:, :, n * W : (n + 1) * W]
+                live["next"] += 1
 
         def nm(u):
             return "%s%d%d" % u
@@ -84,10 +110,23 @@ def tile_qlinear_kernel(tc, x, r_weight, i_weight, j_weight, k_weight, bias, gra
             codes[u] = keep.tile([P, W], U32, name="cod" + nm(u), align_bytes=64)
             scales[u] = keep.tile([P, W], U8, name="scl" + nm(u), align_bytes=64)
 
-        def regroup(u, fs):
+        def copied(u):
+            if u[0] == "x":
+                live["x"] -= 1
+                pump()
+
+        def regroup(u):
             new_unit(u)
-            copy_part("S", u, 0, fs)
-            copy_part("V", u, fs, W)
+            copy_part("S", u, 0, FS)
+            copy_part("V", u, FS, W)
+            copied(u)
+
+        def fine_copy(u):
+            new_unit(u)
+            copy_part("S", u, 2 * P, W)
+            copy_part("V", u, 0, P)
+            copy_part("V", u, P, 2 * P)
+            copied(u)
 
         def quantise(u, a=0, b=W):
             fmt = E4M3 if u[0] == "x" else E5M2
@@ -97,135 +136,156 @@ def tile_qlinear_kernel(tc, x, r_weight, i_weight, j_weight, k_weight, bias, gra
                 in_=grp[u][:, a:b, :].rearrange("p w t -> p (w t)"),
             )
 
-        def mx_pass(r, c, m, n):
+        segs = {0: (LO, 0, A - 1), 1: (HI, 0, PASSES - 1), 2: (LO, A, PASSES - 1)}
+
+        def mx_pass(seg, c, m, n):
+            r, c0, c1 = segs[seg]
+            if c == c0:
+                acc[(seg, m, n)] = psum.tile([P, W], F32, name="acc%d%d%d" % (seg, m, n), tag="acc%d%d" % (m, n))
             xu = ("x", r, c)
             gu = ("g", n, c)
             nc.tensor.matmul_mx(
-                out=acc[(r, m, n)][:],
+                out=acc[(seg, m, n)][:],
                 lhsT=codes[xu][:, m * P : (m + 1) * P].bitcast(E4M3),
                 lhsT_scale=scales[xu][:, m * P : (m + 1) * P],
                 rhs=codes[gu][:].bitcast(E5M2),
                 rhs_scale=scales[gu][:],
-                start=(c == 0),
-                stop=(c == PASSES - 1),
+                start=(c == c0),
+                stop=(c == c1),
             )
 
-        def new_acc(r, m, n):
-            acc[(r, m, n)] = psum.tile([P, W], F32, name="acc%d%d%d" % (r, m, n), tag="acc%d%d" % (m, n))
+        def row(seg, c, m):
+            for n in range(NT):
+                mx_pass(seg, c, m, n)
 
-        osb = {}
+        def from_psum(eng, dst, s):
+            if eng == "S":
+                nc.scalar.copy(out=dst, in_=s)
+            else:
+                nc.vector.tensor_copy(out=dst, in_=s)
 
-        def evac(eng, r, m, n):
+        def spill(m):
+            for n, eng in ((0, "S"), (1, "V")):
+                spl[(m, n)] = keep.tile([P, W], F32, name="spl%d%d" % (m, n))
+                from_psum(eng, spl[(m, n)][:], acc[(0, m, n)][:])
+
+        def out_tile(r, m):
             if (r, m) not in osb:
                 osb[(r, m)] = outp.tile([P, NT * W], F32, name="osb%d%d" % (r, m), tag="osb")
-            dst = osb[(r, m)][:, n * W : (n + 1) * W]
-            if eng == "S":
-                nc.scalar.copy(out=dst, in_=acc[(r, m, n)][:])
-            else:
-                nc.vector.tensor_copy(out=dst, in_=acc[(r, m, n)][:])
+            return osb[(r, m)]
 
-        def store(r, m, n=None):
-            row = (r * MT + m) * P
-            if n is None:
-                nc.sync.dma_start(out=out[row : row + P, :], in_=osb[(r, m)][:])
-            else:
-                nc.sync.dma_start(
-                    out=out[row : row + P, n * W : (n + 1) * W], in_=osb[(r, m)][:, n * W : (n + 1) * W]
-                )
+        def store(r, m, a=0, b=NT * W):
+            row0 = (r * MT + m) * P
+            nc.sync.dma_start(out=out[row0 : row0 + P, a:b], in_=osb[(r, m)][:, a:b])
 
-        units = []
-        for c in range(PASSES):
-            if c < PASSES - 1:
-                load_x(0, c)
-                units.append(("x", 0, c))
-            load_g(c, halves=(c == 0 or c >= PASSES - 2))
-            units.append(("g", 0, c))
-            units.append(("g", 1, c))
-        load_x(0, PASSES - 1)
-        last = ("x", 0, PASSES - 1)
+        def out_hi(m):
+            for n, eng in ((0, "S"), (1, "V")):
+                from_psum(eng, out_tile(HI, m)[:, n * W : (n + 1) * W], acc[(1, m, n)][:])
+            store(HI, m)
 
-        for m in range(MT):
-            for n in range(NT):
-                new_acc(0, m, n)
+        def add_lo(m, n):
+            nc.vector.tensor_tensor(
+                out=out_tile(LO, m)[:, n * W : (n + 1) * W],
+                in0=acc[(2, m, n)][:],
+                in1=spl[(m, n)][:],
+                op=mybir.AluOpType.add,
+            )
 
         ready = set()
         issued = set()
+        pos = {"i": 0, "pend": None}
 
-        def passes_now():
-            for c in range(PASSES):
+        def bulk_passes(seg):
+            r, c0, c1 = segs[seg]
+            for c in range(c0, c1):
                 for n in range(NT):
-                    if (c, n) not in issued and ("x", 0, c) in ready and ("g", n, c) in ready:
-                        issued.add((c, n))
-                        for m in range(MT):
-                            mx_pass(0, c, m, n)
+                    if (seg, c, n) in issued or ("x", r, c) not in ready or ("g", n, c) not in ready:
+                        continue
+                    if n == 1 and (seg, c, 0) not in issued:
+                        continue
+                    issued.add((seg, c, n))
+                    for m in range(MT):
+                        mx_pass(seg, c, m, n)
 
-        for i, u in enumerate(units):
-            regroup(u, FS if i < len(units) - 2 else FS_END)
-            if u[0] == "x":
-                load_x(1, u[2])
-            if i >= 1:
-                quantise(units[i - 1])
-                ready.add(units[i - 1])
-                passes_now()
+        def flush(seg):
+            if pos["pend"] is not None:
+                quantise(pos["pend"])
+                ready.add(pos["pend"])
+                bulk_passes(seg)
+                pos["pend"] = None
 
-        new_unit(last)
-        copy_part("S", last, 2 * P, W)
-        copy_part("V", last, 0, P)
-        quantise(units[-1])
-        copy_part("V", last, P, 2 * P)
-        load_x(1, PASSES - 1)
-        c7 = PASSES - 1
-        quantise(last, 0, P)
-        mx_pass(0, c7, 0, 0)
-        mx_pass(0, c7, 0, 1)
-        quantise(last, P, 2 * P)
-        mx_pass(0, c7, 1, 0)
-        mx_pass(0, c7, 1, 1)
-        quantise(last, 2 * P, W)
-        for m in (2, 3):
-            mx_pass(0, c7, m, 0)
-            mx_pass(0, c7, m, 1)
+        def stream_until(stop_unit, seg):
+            while units[pos["i"]] != stop_unit:
+                u = units[pos["i"]]
+                regroup(u)
+                flush(seg)
+                pos["pend"] = u
+                pos["i"] += 1
 
-        hu = [("x", 1, c) for c in range(PASSES)]
-        regroup(hu[0], FS_END)
-        evac("S", 0, 0, 0)
-        evac("V", 0, 0, 1)
-        store(0, 0)
-        quantise(hu[0])
-        evac("S", 0, 1, 0)
-        evac("V", 0, 1, 1)
-        store(0, 1)
-        regroup(hu[1], FS)
-        evac("S", 0, 2, 0)
-        evac("V", 0, 2, 1)
-        store(0, 2)
-        quantise(hu[1])
-        evac("S", 0, 3, 0)
-        evac("V", 0, 3, 1)
-        store(0, 3)
+        def fine_q(u):
+            quantise(u, 0, P)
+            quantise(u, P, 2 * P)
+            quantise(u, 2 * P, W)
+            ready.add(u)
+
+        def change(seg, free):
+            c1 = segs[seg][2]
+            u = units[pos["i"]]
+            fine_copy(u)
+            flush(seg)
+            quantise(u, 0, P)
+            row(seg, c1, 0)
+            quantise(u, P, 2 * P)
+            row(seg, c1, 1)
+            quantise(u, 2 * P, W)
+            row(seg, c1, 2)
+            row(seg, c1, 3)
+            v0 = units[pos["i"] + 1]
+            fine_copy(v0)
+            fine_q(v0)
+            free(0)
+            free(1)
+            pos["i"] += 2
+
+        pump()
+        stream_until(("x", LO, A - 1), 0)
+        change(0, spill)
+        row(1, 0, 0)
+        row(1, 0, 1)
+        v1 = units[pos["i"]]
+        pos["i"] += 1
+        fine_copy(v1)
+        fine_q(v1)
+        row(1, 1, 0)
+        row(1, 1, 1)
+        spill(2)
+        spill(3)
+        for c in (0, 1):
+            row(1, c, 2)
+            row(1, c, 3)
+            issued.add((1, c, 0))
+            issued.add((1, c, 1))
+        stream_until(("x", HI, PASSES - 1), 1)
+        change(1, out_hi)
+        row(2, A, 0)
+        row(2, A, 1)
+        v1 = units[pos["i"]]
+        pos["i"] += 1
+        fine_copy(v1)
+        fine_q(v1)
+        out_hi(2)
+        out_hi(3)
+        row(2, A, 2)
+        row(2, A, 3)
+        for u in units[pos["i"] :]:
+            fine_copy(u)
+            fine_q(u)
         for m in range(MT):
             for n in range(NT):
-                new_acc(1, m, n)
-        for c in range(2):
-            for m in range(MT):
-                for n in range(NT):
-                    mx_pass(1, c, m, n)
-
-        regroup(hu[2], FS)
-        for c in range(3, PASSES):
-            regroup(hu[c], FS)
-            quantise(hu[c - 1])
-            if c - 1 < K_OUTER2:
-                for m in range(MT):
-                    for n in range(NT):
-                        mx_pass(1, c - 1, m, n)
-        quantise(hu[PASSES - 1])
-        for m in range(MT):
-            for n in range(NT):
-                for c in range(K_OUTER2, PASSES):
-                    mx_pass(1, c, m, n)
-                evac("S" if n == 0 else "V", 1, m, n)
+                for c in range(A + 1, PASSES):
+                    mx_pass(2, c, m, n)
+                add_lo(m, n)
                 if m == MT - 1:
-                    store(1, m, n)
+                    store(LO, m, n * W, (n + 1) * W)
             if m < MT - 1:
-                store(1, m)
+                store(LO, m)

@@ -89,7 +89,12 @@ def tile_qlinear_kernel(tc, x, r_weight, i_weight, j_weight, k_weight, bias, gra
                     c = ld[1]
                     h, q = divmod(c, 4)
                     t = raw.tile([P, J, FEAT], BF16, name="graw%d" % c, tag="graw")
-                    nc.sync.dma_start(out=t[:], in_=gv[h, :, :, q * FEAT : (q + 1) * FEAT])
+                    if c == PASSES - 1:
+                        for n in range(NT):
+                            col = q * FEAT + n * W
+                            nc.sync.dma_start(out=t[:, :, n * W : (n + 1) * W], in_=gv[h, :, :, col : col + W])
+                    else:
+                        nc.sync.dma_start(out=t[:], in_=gv[h, :, :, q * FEAT : (q + 1) * FEAT])
                     for n in range(NT):
                         src[("g", n, c)] = t[:, :, n * W : (n + 1) * W]
                 live["next"] += 1
@@ -179,7 +184,7 @@ def tile_qlinear_kernel(tc, x, r_weight, i_weight, j_weight, k_weight, bias, gra
             nc.sync.dma_start(out=out[row0 : row0 + P, a:b], in_=osb[(r, m)][:, a:b])
 
         def out_hi(m):
-            for n, eng in ((0, "S"), (1, "V")):
+            for n, eng in ((0, "S"), (1, "V" if m < 2 else "S")):
                 from_psum(eng, out_tile(HI, m)[:, n * W : (n + 1) * W], acc[(1, m, n)][:])
             store(HI, m)
 
@@ -271,8 +276,12 @@ def tile_qlinear_kernel(tc, x, r_weight, i_weight, j_weight, k_weight, bias, gra
         row(2, A, 1)
         v1 = units[pos["i"]]
         pos["i"] += 1
-        fine_copy(v1)
-        fine_q(v1)
+        new_unit(v1)
+        copy_part("V", v1, 0, 2 * P)
+        copy_part("V", v1, 2 * P, W)
+        copied(v1)
+        quantise(v1, 0, 2 * P)
+        quantise(v1, 2 * P, W)
         out_hi(2)
         out_hi(3)
         row(2, A, 2)

@@ -33,7 +33,6 @@ def tile_qlinear_kernel(tc, x, r_weight, i_weight, j_weight, k_weight, bias, gra
     gv = grad_out.rearrange("h (p j) c -> h p j c", j=J)
 
     with ExitStack() as ctx:
-        ctx.enter_context(tc.manual_schedule())
         raw = ctx.enter_context(tc.tile_pool(name="raw", bufs=8))
         stage = ctx.enter_context(tc.tile_pool(name="stage", bufs=GRP_BUFS))
         keep = ctx.enter_context(tc.tile_pool(name="keep", bufs=1))

from contextlib import ExitStack

import concourse.mybir as mybir

BF16 = mybir.dt.bfloat16
F32 = mybir.dt.float32
U32 = mybir.dt.uint32
U8 = mybir.dt.uint8
E4M3 = mybir.dt.float8_e4m3fn_x4
E5M2 = mybir.dt.float8_e5m2_x4

P = 128
J = 4
W = 512
FEAT = 1024
PASSES = 8
MT = 4
NT = 2
LO, HI = 0, 1

FLOPS = 2 * 4096 * 1024 * 1024
BYTES = 2 * (1024 * 4096 * 2) + 1024 * 1024 * 4

A = 5
FS = 280
GRP_BUFS = 5
XRAW_BUFS = 8


def tile_qlinear_kernel(tc, x, r_weight, i_weight, j_weight, k_weight, bias, grad_out, out):
    nc = tc.nc
    xv = x.rearrange("h (p j) c -> h p j c", j=J)
    gv = grad_out.rearrange("h (p j) c -> h p j c", j=J)

    with ExitStack() as ctx:
        raw = ctx.enter_context(tc.tile_pool(name="raw", bufs=8))
        stage = ctx.enter_context(tc.tile_pool(name="stage", bufs=GRP_BUFS))
        keep = ctx.enter_context(tc.tile_pool(name="keep", bufs=1))
        outp = ctx.enter_context(tc.tile_pool(name="outp", bufs=4))
        psum = ctx.enter_context(tc.psum_pool(name="psum", bufs=1))

        src = {}
        grp = {}
        codes = {}
        scales = {}
        acc = {}
        spl = {}
        osb = {}

        units = []
        pending = []
        for c in range(A):
            if c < A - 1:
                pending.append(("x", LO, c))
            pending.append(("g", c))
        pending.append(("x", LO, A - 1))
        for c in range(A):
            pending.append(("x", HI, c))
        for c in range(A, PASSES):
            if c < PASSES - 1:
                pending.append(("x", HI, c))
            pending.append(("g", c))
        pending.append(("x", HI, PASSES - 1))
        for c in range(A, PASSES):
            pending.append(("x", LO, c))
        for ld in pending:
            if ld[0] == "x":
                units.append(ld)
            else:
                units.append(("g", 0, ld[1]))
                units.append(("g", 1, ld[1]))
        live = {"x": 0, "next": 0}

        def pump():
            while live["next"] < len(pending):
                ld = pending[live["next"]]
                if ld[0] == "x":
                    if live["x"] == XRAW_BUFS:
                        return
                    live["x"] += 1
                    r, c = ld[1], ld[2]
                    h, q = divmod(c, 4)
                    t = raw.tile([P, J, W], BF16, name="xraw%d%d" % (r, c), tag="xraw")
                    col = q * FEAT + r * W
                    nc.sync.dma_start(out=t[:], in_=xv[h, :, :, col : col + W])
                    src[ld] = t[:]
                else:
                    c = ld[1]
                    h, q = divmod(c, 4)
                    t = raw.tile([P, J, FEAT], BF16, name="graw%d" % c, tag="graw")
                    if c == PASSES - 1:
                        for n in range(NT):
                            col = q * FEAT + n * W
                            nc.sync.dma_start(out=t[:, :, n * W : (n + 1) * W], in_=gv[h, :, :, col : col + W])
                    else:
                        nc.sync.dma_start(out=t[:], in_=gv[h, :, :, q * FEAT : (q + 1) * FEAT])
                    for n in range(NT):
                        src[("g", n, c)] = t[:, :, n * W : (n + 1) * W]
                live["next"] += 1

        def nm(u):
            return "%s%d%d" % u

        def copy_part(eng, u, a, b):
            dst = grp[u][:, a:b, :].rearrange("p (c i) t -> p c t i", i=4)
            s = src[u][:, :, a:b].rearrange("p t (c i) -> p c t i", i=4)
            if eng == "S":
                nc.scalar.copy(out=dst, in_=s)
            else:
                nc.vector.tensor_copy(out=dst, in_=s)

        def new_unit(u):
            grp[u] = stage.tile([P, W, J], BF16, name="grp" + nm(u), tag="grp", align_bytes=64)
            codes[u] = keep.tile([P, W], U32, name="cod" + nm(u), align_bytes=64)
            scales[u] = keep.tile([P, W], U8, name="scl" + nm(u), align_bytes=64)

        def copied(u):
            if u[0] == "x":
                live["x"] -= 1
                pump()

        def regroup(u):
            new_unit(u)
            copy_part("S", u, 0, FS)
            copy_part("V", u, FS, W)
            copied(u)

        def fine_copy(u):
            new_unit(u)
            copy_part("S", u, 2 * P, W)
            copy_part("V", u, 0, P)
            copy_part("V", u, P, 2 * P)
            copied(u)

        def quantise(u, a=0, b=W):
            fmt = E4M3 if u[0] == "x" else E5M2
            nc.vector.quantize_mx(
                out=codes[u][:, a:b].bitcast(fmt),
                scales=scales[u][:, a:b],
                in_=grp[u][:, a:b, :].rearrange("p w t -> p (w t)"),
            )

        segs = {0: (LO, 0, A - 1), 1: (HI, 0, PASSES - 1), 2: (LO, A, PASSES - 1)}

        def mx_pass(seg, c, m, n):
            r, c0, c1 = segs[seg]
            if c == c0:
                acc[(seg, m, n)] = psum.tile([P, W], F32, name="acc%d%d%d" % (seg, m, n), tag="acc%d%d" % (m, n))
            xu = ("x", r, c)
            gu = ("g", n, c)
            nc.tensor.matmul_mx(
                out=acc[(seg, m, n)][:],
                lhsT=codes[xu][:, m * P : (m + 1) * P].bitcast(E4M3),
                lhsT_scale=scales[xu][:, m * P : (m + 1) * P],
                rhs=codes[gu][:].bitcast(E5M2),
                rhs_scale=scales[gu][:],
                start=(c == c0),
                stop=(c == c1),
            )

        def row(seg, c, m):
            for n in range(NT):
                mx_pass(seg, c, m, n)

        def from_psum(eng, dst, s):
            if eng == "S":
                nc.scalar.copy(out=dst, in_=s)
            else:
                nc.vector.tensor_copy(out=dst, in_=s)

        def spill(m):
            for n, eng in ((0, "S"), (1, "V")):
                spl[(m, n)] = keep.tile([P, W], F32, name="spl%d%d" % (m, n))
                from_psum(eng, spl[(m, n)][:], acc[(0, m, n)][:])

        def out_tile(r, m):
            if (r, m) not in osb:
                osb[(r, m)] = outp.tile([P, NT * W], F32, name="osb%d%d" % (r, m), tag="osb")
            return osb[(r, m)]

        def store(r, m, a=0, b=NT * W):
            row0 = (r * MT + m) * P
            nc.sync.dma_start(out=out[row0 : row0 + P, a:b], in_=osb[(r, m)][:, a:b])

        def out_hi(m):
            for n, eng in ((0, "S"), (1, "V" if m < 2 else "S")):
                from_psum(eng, out_tile(HI, m)[:, n * W : (n + 1) * W], acc[(1, m, n)][:])
            store(HI, m)

        def add_lo(m, n):
            nc.vector.tensor_tensor(
                out=out_tile(LO, m)[:, n * W : (n + 1) * W],
                in0=acc[(2, m, n)][:],
                in1=spl[(m, n)][:],
                op=mybir.AluOpType.add,
            )

        ready = set()
        issued = set()
        pos = {"i": 0, "pend": None}

        def bulk_passes(seg):
            r, c0, c1 = segs[seg]
            for c in range(c0, c1):
                for n in range(NT):
                    if (seg, c, n) in issued or ("x", r, c) not in ready or ("g", n, c) not in ready:
                        continue
                    if n == 1 and (seg, c, 0) not in issued:
                        continue
                    issued.add((seg, c, n))
                    for m in range(MT):
                        mx_pass(seg, c, m, n)

        def flush(seg):
            if pos["pend"] is not None:
                quantise(pos["pend"])
                ready.add(pos["pend"])
                bulk_passes(seg)
                pos["pend"] = None

        def stream_until(stop_unit, seg):
            while units[pos["i"]] != stop_unit:
                u = units[pos["i"]]
                regroup(u)
                flush(seg)
                pos["pend"] = u
                pos["i"] += 1

        def fine_q(u):
            quantise(u, 0, P)
            quantise(u, P, 2 * P)
            quantise(u, 2 * P, W)
            ready.add(u)

        def change(seg, free):
            c1 = segs[seg][2]
            u = units[pos["i"]]
            fine_copy(u)
            flush(seg)
            quantise(u, 0, P)
            row(seg, c1, 0)
            quantise(u, P, 2 * P)
            row(seg, c1, 1)
            quantise(u, 2 * P, W)
            row(seg, c1, 2)
            row(seg, c1, 3)
            v0 = units[pos["i"] + 1]
            fine_copy(v0)
            fine_q(v0)
            free(0)
            free(1)
            pos["i"] += 2

        pump()
        stream_until(("x", LO, A - 1), 0)
        change(0, spill)
        row(1, 0, 0)
        row(1, 0, 1)
        v1 = units[pos["i"]]
        pos["i"] += 1
        fine_copy(v1)
        fine_q(v1)
        row(1, 1, 0)
        row(1, 1, 1)
        spill(2)
        spill(3)
        for c in (0, 1):
            row(1, c, 2)
            row(1, c, 3)
            issued.add((1, c, 0))
            issued.add((1, c, 1))
        stream_until(("x", HI, PASSES - 1), 1)
        change(1, out_hi)
        row(2, A, 0)
        row(2, A, 1)
        v1 = units[pos["i"]]
        pos["i"] += 1
        new_unit(v1)
        copy_part("V", v1, 0, 2 * P)
        copy_part("V", v1, 2 * P, W)
        copied(v1)
        quantise(v1, 0, 2 * P)
        quantise(v1, 2 * P, W)
        out_hi(2)
        out_hi(3)
        row(2, A, 2)
        row(2, A, 3)
        for u in units[pos["i"] :]:
            fine_copy(u)
            fine_q(u)
        for m in range(MT):
            for n in range(NT):
                for c in range(A + 1, PASSES):
                    mx_pass(2, c, m, n)
                add_lo(m, n)
                if m == MT - 1:
                    store(LO, m, n * W, (n + 1) * W)
            if m < MT - 1:
                store(LO, m)
